import numpy as np
import ml_dtypes

BF16 = ml_dtypes.bfloat16


def bf(x):
    return np.asarray(x, np.float32).astype(BF16)


def f32(x):
    return np.asarray(x, np.float32)


def f64(x):
    return np.asarray(x).astype(np.float64)


def striped(idx):
    return np.tile(idx.reshape(-1, 16).T, (8, 1))


V, E, E2, HA, HC, L, P, SIDES, N = 4096, 128, 256, 512, 1024, 256, 3, 2, 1536


def relu(v):
    return np.maximum(v, 0.0)


def setup_inputs():
    return {
        "table": bf(np.random.standard_normal((V, E))),
        "w1a": bf(np.random.standard_normal((E, HA)) / np.sqrt(E)),
        "b1a": f32(0.1 * np.random.standard_normal((HA, 1))),
        "w2a": bf(0.5 * np.random.standard_normal((HA, HA)) / np.sqrt(HA)),
        "b2a": f32(0.1 * np.random.standard_normal((HA, 1))),
        "w1c": bf(np.random.standard_normal((E2, HC)) / np.sqrt(E)),
        "b1c": f32(0.1 * np.random.standard_normal((HC, 1))),
        "w2c": bf(np.sqrt(2.0) * np.random.standard_normal((HC, HC)) / np.sqrt(HC)),
        "b2c": f32(0.1 * np.random.standard_normal((HC, 1))),
        "offs": striped(np.random.permutation(V)[:N]),
    }


def reference(table, w1a, b1a, w2a, b2a, w1c, b1c, w2c, b2c, offs):
    idx = offs[:16].T.reshape(-1)
    x = f64(table)[idx].T
    a1 = relu(f64(w1a).T @ x + f64(b1a))
    h = relu(f64(w2a).T @ a1 + f64(b2a))
    ctx = np.zeros((E, N))
    for r in range(SIDES * P):
        q = r ^ 1
        me = slice(r * L, (r + 1) * L)
        it = slice(q * L, (q + 1) * L)
        sc = h[:, me].T @ h[:, it]
        ex = np.exp(sc - sc.max(axis=1, keepdims=True))
        att = ex / ex.sum(axis=1, keepdims=True)
        ctx[:, me] = x[:, it] @ att.T
    c1 = relu(f64(w1c).T @ np.concatenate([x, ctx], axis=0) + f64(b1c))
    return relu(f64(w2c).T @ c1 + f64(b2c))

@@ -1,0 +1,206 @@
+from contextlib import ExitStack
+
+import concourse.mybir as mybir
+from concourse.masks import make_identity
+
+BF16, F32, U16 = mybir.dt.bfloat16, mybir.dt.float32, mybir.dt.uint16
+ACT = mybir.ActivationFunctionType
+ALU = mybir.AluOpType
+AXIS_X = mybir.AxisListType.X
+
+P = 128
+V, E, HA, HC = 4096, 128, 512, 1024
+N, PIECE, BLOCK = 1536, 512, 256
+PAIRS, BLOCKS = N // PIECE, N // BLOCK
+KA, KC = HA // P, HC // P
+FLIP = 512
+
+FLOPS = 2 * N * (E * HA + HA * HA + 2 * E * HC + HC * HC) + BLOCKS * 2 * BLOCK * BLOCK * (HA + E)
+
+B1A, B2A, B1C, B2C = 0, KA, 2 * KA, 2 * KA + KC
+
+
+def tile_decomposableattention_b_kernel(
+    tc, table, w1a, b1a, w2a, b2a, w1c, b1c, w2c, b2c, offs, out
+):
+    nc = tc.nc
+    with ExitStack() as stack:
+        held = stack.enter_context(tc.tile_pool(name="held", bufs=1))
+        soft = stack.enter_context(tc.tile_pool(name="soft", bufs=3))
+        stage = stack.enter_context(tc.tile_pool(name="stage", bufs=4))
+        psum_acc = stack.enter_context(tc.psum_pool(name="psum_acc", bufs=4))
+        psum_sc = stack.enter_context(tc.psum_pool(name="psum_sc", bufs=2))
+        psum_flip = stack.enter_context(tc.psum_pool(name="psum_flip", bufs=2))
+
+        offsets = held.tile([P, N // 16], U16, name="offsets")
+        nc.sync.dma_start(offsets[:], offs)
+
+        rows = held.tile([P, V // P, E], BF16, name="rows")
+        table_blocks = table.rearrange("(b p) e -> p b e", p=P)
+        for c in range(4):
+            blocks = slice(c * 8, (c + 1) * 8)
+            nc.sync.dma_start(rows[:, blocks, :], table_blocks[:, blocks, :])
+
+        w1a_sb = held.tile([P, HA], BF16, name="w1a_sb")
+        nc.scalar.dma_start(w1a_sb[:], w1a)
+
+        bias_rows = held.tile([P, P], F32, name="bias_rows")
+        nc.vector.memset(bias_rows[:], 0.0)
+        for column, vector, count in ((B1A, b1a, KA), (B2A, b2a, KA), (B1C, b1c, KC), (B2C, b2c, KC)):
+            nc.scalar.dma_start(
+                bias_rows[column : column + count, :], vector.rearrange("(m p) o -> m (p o)", p=P)
+            )
+
+        w2a_sb = held.tile([P, KA, HA], BF16, name="w2a_sb")
+        nc.sync.dma_start(w2a_sb[:], w2a.rearrange("(k p) m -> p k m", p=P))
+        w1c_sb = held.tile([P, 2, HC], BF16, name="w1c_sb")
+        nc.sync.dma_start(w1c_sb[:], w1c.rearrange("(k p) m -> p k m", p=P))
+        w2c_sb = held.tile([P, KC, HC], BF16, name="w2c_sb")
+        nc.sync.dma_start(w2c_sb[:], w2c.rearrange("(k p) m -> p k m", p=P))
+
+        ident_bf = held.tile([P, P], BF16, name="ident_bf")
+        make_identity(nc, ident_bf[:])
+        ident_f32 = held.tile([P, P], F32, name="ident_f32")
+        make_identity(nc, ident_f32[:])
+
+        warm = held.tile([P, 1], F32, name="warm")
+        nc.vector.memset(warm[:], 0.0)
+        nc.scalar.activation(warm[:], warm[:], ACT.Exp)
+
+        turn = [0]
+
+        def next_engine_is_scalar():
+            turn[0] += 1
+            return turn[0] % 2 == 1
+
+        def copy_out(dst, src):
+            if next_engine_is_scalar():
+                nc.scalar.copy(dst, src)
+            else:
+                nc.vector.tensor_copy(dst, src)
+
+        def relu_out(dst, src, bias_column):
+            bias = biases[:, bias_column : bias_column + 1]
+            if next_engine_is_scalar():
+                nc.scalar.activation(dst, src, ACT.Relu, bias=bias)
+            else:
+                nc.vector.tensor_scalar(dst, src, bias, 0.0, op0=ALU.add, op1=ALU.max)
+
+        bias_ps = psum_acc.tile([P, P], F32, tag="acc")
+        nc.tensor.transpose(bias_ps[:], bias_rows[:], ident_f32[:])
+        biases = held.tile([P, B2C + KC], F32, name="biases")
+        nc.vector.tensor_copy(biases[:], bias_ps[:, : B2C + KC])
+
+        tableT = held.tile([P, V], BF16, name="tableT")
+        for f in range(V // FLIP):
+            flip_ps = psum_flip.tile([P, FLIP], BF16, tag="flip")
+            for i in range(FLIP // P):
+                nc.tensor.transpose(
+                    flip_ps[:, i * P : (i + 1) * P], rows[:, f * (FLIP // P) + i, :], ident_bf[:]
+                )
+            copy_out(tableT[:, f * FLIP : (f + 1) * FLIP], flip_ps[:])
+
+        a1 = held.tile([P, KA, N], BF16, name="a1")
+        x = held.tile([P, N], BF16, name="x")
+        for p in range(PAIRS):
+            cols = slice(p * PIECE, (p + 1) * PIECE)
+            looked_up = tableT[:].indirect(offsets[:, p * (PIECE // 16) : (p + 1) * (PIECE // 16)])
+            for m in range(KA):
+                a1_ps = psum_acc.tile([P, PIECE], F32, tag="acc")
+                nc.tensor.matmul(a1_ps[:], w1a_sb[:, m * P : (m + 1) * P], looked_up)
+                relu_out(a1[:, m, cols], a1_ps[:], B1A + m)
+            x_ps = psum_acc.tile([P, PIECE], F32, tag="acc")
+            nc.tensor.matmul(x_ps[:], ident_bf[:], looked_up)
+            copy_out(x[:, cols], x_ps[:])
+
+        xT = held.tile([P, N], BF16, name="xT")
+        for p in range(PAIRS):
+            xT_ps = psum_flip.tile([P, PIECE], BF16, tag="flip")
+            for i in range(PIECE // P):
+                group = slice(p * PIECE + i * P, p * PIECE + (i + 1) * P)
+                nc.tensor.transpose(xT_ps[:, i * P : (i + 1) * P], x[:, group], ident_bf[:])
+            copy_out(xT[:, p * PIECE : (p + 1) * PIECE], xT_ps[:])
+
+        h = held.tile([P, KA, N], BF16, name="h")
+        for p in range(PAIRS):
+            cols = slice(p * PIECE, (p + 1) * PIECE)
+            for m in range(KA):
+                h_ps = psum_acc.tile([P, PIECE], F32, tag="acc")
+                for k in range(KA):
+                    nc.tensor.matmul(
+                        h_ps[:], w2a_sb[:, k, m * P : (m + 1) * P], a1[:, k, cols],
+                        start=(k == 0), stop=(k == KA - 1),
+                    )
+                relu_out(h[:, m, cols], h_ps[:], B2A + m)
+
+        ctx = held.tile([P, N], BF16, name="ctx")
+        halves = BLOCK // P
+        for r in range(BLOCKS):
+            partner = r ^ 1
+            theirs = slice(partner * BLOCK, (partner + 1) * BLOCK)
+
+            sc_ps = psum_sc.tile([P, halves, BLOCK], F32, tag="sc")
+            for g in range(halves):
+                mine = slice(r * BLOCK + g * P, r * BLOCK + (g + 1) * P)
+                for k in range(KA):
+                    nc.tensor.matmul(
+                        sc_ps[:, g, :], h[:, k, mine], h[:, k, theirs],
+                        start=(k == 0), stop=(k == KA - 1),
+                    )
+
+            neg_max = soft.tile([P, halves], F32, tag="neg_max")
+            nc.vector.reduce_max(neg_max[:], sc_ps[:], axis=AXIS_X, negate=True)
+            expo = soft.tile([P, halves, BLOCK], F32, tag="expo")
+            sums = soft.tile([P, halves], F32, tag="sums")
+            for g in range(halves):
+                nc.scalar.activation(
+                    expo[:, g, :], sc_ps[:, g, :], ACT.Exp,
+                    bias=neg_max[:, g : g + 1], accum_out=sums[:, g : g + 1],
+                )
+            inverse = soft.tile([P, halves], F32, tag="inverse")
+            nc.vector.reciprocal(inverse[:], sums[:])
+            att = soft.tile([P, halves, BLOCK], BF16, tag="att")
+            for g in range(halves):
+                nc.vector.tensor_scalar(
+                    att[:, g, :], expo[:, g, :], inverse[:, g : g + 1], None, op0=ALU.mult
+                )
+
+            attT_ps = psum_flip.tile([P, halves, BLOCK], BF16, tag="flip")
+            for u in range(halves):
+                for g in range(halves):
+                    nc.tensor.transpose(
+                        attT_ps[:, u, g * P : (g + 1) * P], att[:, g, u * P : (u + 1) * P], ident_bf[:]
+                    )
+            attT = soft.tile([P, halves, BLOCK], BF16, tag="attT")
+            copy_out(attT[:], attT_ps[:])
+
+            ctx_ps = psum_acc.tile([P, BLOCK], F32, tag="acc")
+            for u in range(halves):
+                their_group = slice(partner * BLOCK + u * P, partner * BLOCK + (u + 1) * P)
+                nc.tensor.matmul(
+                    ctx_ps[:], xT[:, their_group], attT[:, u, :],
+                    start=(u == 0), stop=(u == halves - 1),
+                )
+            copy_out(ctx[:, r * BLOCK : (r + 1) * BLOCK], ctx_ps[:])
+
+        c1 = held.tile([P, KC, N], BF16, name="c1")
+        for p in range(PAIRS):
+            cols = slice(p * PIECE, (p + 1) * PIECE)
+            for m in range(KC):
+                c1_ps = psum_acc.tile([P, PIECE], F32, tag="acc")
+                nc.tensor.matmul(c1_ps[:], w1c_sb[:, 0, m * P : (m + 1) * P], x[:, cols], start=True, stop=False)
+                nc.tensor.matmul(c1_ps[:], w1c_sb[:, 1, m * P : (m + 1) * P], ctx[:, cols], start=False, stop=True)
+                relu_out(c1[:, m, cols], c1_ps[:], B1C + m)
+
+        for p in range(PAIRS):
+            cols = slice(p * PIECE, (p + 1) * PIECE)
+            for m in range(KC):
+                out_ps = psum_acc.tile([P, PIECE], F32, tag="acc")
+                for k in range(KC):
+                    nc.tensor.matmul(
+                        out_ps[:], w2c_sb[:, k, m * P : (m + 1) * P], c1[:, k, cols],
+                        start=(k == 0), stop=(k == KC - 1),
+                    )
+                out_sb = stage.tile([P, PIECE], F32, tag="out_sb")
+                relu_out(out_sb[:], out_ps[:], B2C + m)
+                nc.sync.dma_start(out[m * P : (m + 1) * P, cols], out_sb[:])

@@ -26,11 +26,9 @@ def tile_decomposableattention_b_kernel(
     nc = tc.nc
     with ExitStack() as stack:
         held = stack.enter_context(tc.tile_pool(name="held", bufs=1))
-        soft = stack.enter_context(tc.tile_pool(name="soft", bufs=3))
+        soft = stack.enter_context(tc.tile_pool(name="soft", bufs=4))
         stage = stack.enter_context(tc.tile_pool(name="stage", bufs=4))
-        psum_acc = stack.enter_context(tc.psum_pool(name="psum_acc", bufs=4))
-        psum_sc = stack.enter_context(tc.psum_pool(name="psum_sc", bufs=2))
-        psum_flip = stack.enter_context(tc.psum_pool(name="psum_flip", bufs=2))
+        psum = stack.enter_context(tc.psum_pool(name="psum", bufs=8))
 
         offsets = held.tile([P, N // 16], U16, name="offsets")
         nc.sync.dma_start(offsets[:], offs)
@@ -86,14 +84,14 @@ def tile_decomposableattention_b_kernel(
             else:
                 nc.vector.tensor_scalar(dst, src, bias, 0.0, op0=ALU.add, op1=ALU.max)
 
-        bias_ps = psum_acc.tile([P, P], F32, tag="acc")
+        bias_ps = psum.tile([P, P], F32, tag="bank")
         nc.tensor.transpose(bias_ps[:], bias_rows[:], ident_f32[:])
         biases = held.tile([P, B2C + KC], F32, name="biases")
         nc.vector.tensor_copy(biases[:], bias_ps[:, : B2C + KC])
 
         tableT = held.tile([P, V], BF16, name="tableT")
         for f in range(V // FLIP):
-            flip_ps = psum_flip.tile([P, FLIP], BF16, tag="flip")
+            flip_ps = psum.tile([P, FLIP], BF16, tag="bank")
             for i in range(FLIP // P):
                 nc.tensor.transpose(
                     flip_ps[:, i * P : (i + 1) * P], rows[:, f * (FLIP // P) + i, :], ident_bf[:]
@@ -106,26 +104,28 @@ def tile_decomposableattention_b_kernel(
             cols = slice(p * PIECE, (p + 1) * PIECE)
             looked_up = tableT[:].indirect(offsets[:, p * (PIECE // 16) : (p + 1) * (PIECE // 16)])
             for m in range(KA):
-                a1_ps = psum_acc.tile([P, PIECE], F32, tag="acc")
+                a1_ps = psum.tile([P, PIECE], F32, tag="bank")
                 nc.tensor.matmul(a1_ps[:], w1a_sb[:, m * P : (m + 1) * P], looked_up)
                 relu_out(a1[:, m, cols], a1_ps[:], B1A + m)
-            x_ps = psum_acc.tile([P, PIECE], F32, tag="acc")
+            x_ps = psum.tile([P, PIECE], F32, tag="bank")
             nc.tensor.matmul(x_ps[:], ident_bf[:], looked_up)
             copy_out(x[:, cols], x_ps[:])
 
         xT = held.tile([P, N], BF16, name="xT")
-        for p in range(PAIRS):
-            xT_ps = psum_flip.tile([P, PIECE], BF16, tag="flip")
+
+        def flip_words(p):
+            xT_ps = psum.tile([P, PIECE], BF16, tag="bank")
             for i in range(PIECE // P):
                 group = slice(p * PIECE + i * P, p * PIECE + (i + 1) * P)
                 nc.tensor.transpose(xT_ps[:, i * P : (i + 1) * P], x[:, group], ident_bf[:])
             copy_out(xT[:, p * PIECE : (p + 1) * PIECE], xT_ps[:])
 
         h = held.tile([P, KA, N], BF16, name="h")
-        for p in range(PAIRS):
+
+        def hidden(p):
             cols = slice(p * PIECE, (p + 1) * PIECE)
             for m in range(KA):
-                h_ps = psum_acc.tile([P, PIECE], F32, tag="acc")
+                h_ps = psum.tile([P, PIECE], F32, tag="bank")
                 for k in range(KA):
                     nc.tensor.matmul(
                         h_ps[:], w2a_sb[:, k, m * P : (m + 1) * P], a1[:, k, cols],
@@ -133,13 +133,14 @@ def tile_decomposableattention_b_kernel(
                     )
                 relu_out(h[:, m, cols], h_ps[:], B2A + m)
 
-        ctx = held.tile([P, N], BF16, name="ctx")
         halves = BLOCK // P
-        for r in range(BLOCKS):
-            partner = r ^ 1
-            theirs = slice(partner * BLOCK, (partner + 1) * BLOCK)
+        att_of = {}
+        attT_of = {}
+        ctx = held.tile([P, N], BF16, name="ctx")
 
-            sc_ps = psum_sc.tile([P, halves, BLOCK], F32, tag="sc")
+        def scores(r):
+            theirs = slice((r ^ 1) * BLOCK, ((r ^ 1) + 1) * BLOCK)
+            sc_ps = psum.tile([P, halves, BLOCK], F32, tag="bank")
             for g in range(halves):
                 mine = slice(r * BLOCK + g * P, r * BLOCK + (g + 1) * P)
                 for k in range(KA):
@@ -147,7 +148,6 @@ def tile_decomposableattention_b_kernel(
                         sc_ps[:, g, :], h[:, k, mine], h[:, k, theirs],
                         start=(k == 0), stop=(k == KA - 1),
                     )
-
             neg_max = soft.tile([P, halves], F32, tag="neg_max")
             nc.vector.reduce_max(neg_max[:], sc_ps[:], axis=AXIS_X, negate=True)
             expo = soft.tile([P, halves, BLOCK], F32, tag="expo")
@@ -164,8 +164,11 @@ def tile_decomposableattention_b_kernel(
                 nc.vector.tensor_scalar(
                     att[:, g, :], expo[:, g, :], inverse[:, g : g + 1], None, op0=ALU.mult
                 )
+            att_of[r] = att
 
-            attT_ps = psum_flip.tile([P, halves, BLOCK], BF16, tag="flip")
+        def flip_att(r):
+            att = att_of[r]
+            attT_ps = psum.tile([P, halves, BLOCK], BF16, tag="bank")
             for u in range(halves):
                 for g in range(halves):
                     nc.tensor.transpose(
@@ -173,10 +176,13 @@ def tile_decomposableattention_b_kernel(
                     )
             attT = soft.tile([P, halves, BLOCK], BF16, tag="attT")
             copy_out(attT[:], attT_ps[:])
+            attT_of[r] = attT
 
-            ctx_ps = psum_acc.tile([P, BLOCK], F32, tag="acc")
+        def context(r):
+            attT = attT_of[r]
+            ctx_ps = psum.tile([P, BLOCK], F32, tag="bank")
             for u in range(halves):
-                their_group = slice(partner * BLOCK + u * P, partner * BLOCK + (u + 1) * P)
+                their_group = slice((r ^ 1) * BLOCK + u * P, (r ^ 1) * BLOCK + (u + 1) * P)
                 nc.tensor.matmul(
                     ctx_ps[:], xT[:, their_group], attT[:, u, :],
                     start=(u == 0), stop=(u == halves - 1),
@@ -184,18 +190,38 @@ def tile_decomposableattention_b_kernel(
             copy_out(ctx[:, r * BLOCK : (r + 1) * BLOCK], ctx_ps[:])
 
         c1 = held.tile([P, KC, N], BF16, name="c1")
-        for p in range(PAIRS):
+
+        def compare(p):
             cols = slice(p * PIECE, (p + 1) * PIECE)
             for m in range(KC):
-                c1_ps = psum_acc.tile([P, PIECE], F32, tag="acc")
+                c1_ps = psum.tile([P, PIECE], F32, tag="bank")
                 nc.tensor.matmul(c1_ps[:], w1c_sb[:, 0, m * P : (m + 1) * P], x[:, cols], start=True, stop=False)
                 nc.tensor.matmul(c1_ps[:], w1c_sb[:, 1, m * P : (m + 1) * P], ctx[:, cols], start=False, stop=True)
                 relu_out(c1[:, m, cols], c1_ps[:], B1C + m)
 
+        hidden(0)
+        for p in range(PAIRS):
+            flip_words(p)
+        hidden(1)
+        scores(0)
+        scores(1)
+        hidden(2)
+        for p in range(PAIRS):
+            first, second = 2 * p, 2 * p + 1
+            flip_att(first)
+            flip_att(second)
+            if p + 1 < PAIRS:
+                scores(first + 2)
+            context(first)
+            context(second)
+            if p + 1 < PAIRS:
+                scores(second + 2)
+            compare(p)
+
         for p in range(PAIRS):
             cols = slice(p * PIECE, (p + 1) * PIECE)
             for m in range(KC):
-                out_ps = psum_acc.tile([P, PIECE], F32, tag="acc")
+                out_ps = psum.tile([P, PIECE], F32, tag="bank")
                 for k in range(KC):
                     nc.tensor.matmul(
                         out_ps[:], w2c_sb[:, k, m * P : (m + 1) * P], c1[:, k, cols],

@@ -14,6 +14,7 @@ N, PIECE, BLOCK = 1536, 512, 256
 PAIRS, BLOCKS = N // PIECE, N // BLOCK
 KA, KC = HA // P, HC // P
 FLIP = 512
+PER = FLIP // P
 
 FLOPS = 2 * N * (E * HA + HA * HA + 2 * E * HC + HC * HC) + BLOCKS * 2 * BLOCK * BLOCK * (HA + E)
 
@@ -33,11 +34,10 @@ def tile_decomposableattention_b_kernel(
         offsets = held.tile([P, N // 16], U16, name="offsets")
         nc.sync.dma_start(offsets[:], offs)
 
-        rows = held.tile([P, V // P, E], BF16, name="rows")
-        table_blocks = table.rearrange("(b p) e -> p b e", p=P)
-        for c in range(4):
-            blocks = slice(c * 8, (c + 1) * 8)
-            nc.sync.dma_start(rows[:, blocks, :], table_blocks[:, blocks, :])
+        rows = held.tile([P, V // FLIP, PER * E], BF16, name="rows")
+        table_chunks = table.rearrange("(c p i) e -> p c (i e)", p=P, i=PER)
+        for c in range(V // FLIP):
+            nc.sync.dma_start(rows[:, c, :], table_chunks[:, c, :])
 
         w1a_sb = held.tile([P, HA], BF16, name="w1a_sb")
         nc.scalar.dma_start(w1a_sb[:], w1a)
@@ -90,13 +90,14 @@ def tile_decomposableattention_b_kernel(
         nc.vector.tensor_copy(biases[:], bias_ps[:, : B2C + KC])
 
         tableT = held.tile([P, V], BF16, name="tableT")
-        for f in range(V // FLIP):
-            flip_ps = psum.tile([P, FLIP], BF16, tag="bank")
-            for i in range(FLIP // P):
-                nc.tensor.transpose(
-                    flip_ps[:, i * P : (i + 1) * P], rows[:, f * (FLIP // P) + i, :], ident_bf[:]
-                )
-            copy_out(tableT[:, f * FLIP : (f + 1) * FLIP], flip_ps[:])
+        for c in range(V // FLIP):
+            flip_ps = psum.tile([P, PER, P], BF16, tag="bank")
+            for i in range(PER):
+                nc.tensor.transpose(flip_ps[:, i, :], rows[:, c, i * E : (i + 1) * E], ident_bf[:])
+            copy_out(
+                tableT[:, c * FLIP : (c + 1) * FLIP].rearrange("d (p i) -> d p i", i=PER),
+                flip_ps[:].rearrange("d i p -> d p i"),
+            )
 
         a1 = held.tile([P, KA, N], BF16, name="a1")
         x = held.tile([P, N], BF16, name="x")

@@ -14,7 +14,6 @@ N, PIECE, BLOCK = 1536, 512, 256
 PAIRS, BLOCKS = N // PIECE, N // BLOCK
 KA, KC = HA // P, HC // P
 FLIP = 512
-PER = FLIP // P
 
 FLOPS = 2 * N * (E * HA + HA * HA + 2 * E * HC + HC * HC) + BLOCKS * 2 * BLOCK * BLOCK * (HA + E)
 
@@ -32,12 +31,12 @@ def tile_decomposableattention_b_kernel(
         psum = stack.enter_context(tc.psum_pool(name="psum", bufs=8))
 
         offsets = held.tile([P, N // 16], U16, name="offsets")
+        rows = held.tile([P, V // P, E], BF16, name="rows")
+        table_blocks = table.rearrange("(b p) e -> p b e", p=P)
+        for c in range(4):
+            blocks = slice(c * 8, (c + 1) * 8)
+            nc.sync.dma_start(rows[:, blocks, :], table_blocks[:, blocks, :])
         nc.sync.dma_start(offsets[:], offs)
-
-        rows = held.tile([P, V // FLIP, PER * E], BF16, name="rows")
-        table_chunks = table.rearrange("(c p i) e -> p c (i e)", p=P, i=PER)
-        for c in range(V // FLIP):
-            nc.sync.dma_start(rows[:, c, :], table_chunks[:, c, :])
 
         w1a_sb = held.tile([P, HA], BF16, name="w1a_sb")
         nc.scalar.dma_start(w1a_sb[:], w1a)
@@ -84,20 +83,19 @@ def tile_decomposableattention_b_kernel(
             else:
                 nc.vector.tensor_scalar(dst, src, bias, 0.0, op0=ALU.add, op1=ALU.max)
 
+        tableT = held.tile([P, V], BF16, name="tableT")
+        for f in range(V // FLIP):
+            flip_ps = psum.tile([P, FLIP], BF16, tag="bank")
+            for i in range(FLIP // P):
+                nc.tensor.transpose(
+                    flip_ps[:, i * P : (i + 1) * P], rows[:, f * (FLIP // P) + i, :], ident_bf[:]
+                )
+            copy_out(tableT[:, f * FLIP : (f + 1) * FLIP], flip_ps[:])
+
         bias_ps = psum.tile([P, P], F32, tag="bank")
         nc.tensor.transpose(bias_ps[:], bias_rows[:], ident_f32[:])
         biases = held.tile([P, B2C + KC], F32, name="biases")
         nc.vector.tensor_copy(biases[:], bias_ps[:, : B2C + KC])
-
-        tableT = held.tile([P, V], BF16, name="tableT")
-        for c in range(V // FLIP):
-            flip_ps = psum.tile([P, PER, P], BF16, tag="bank")
-            for i in range(PER):
-                nc.tensor.transpose(flip_ps[:, i, :], rows[:, c, i * E : (i + 1) * E], ident_bf[:])
-            copy_out(
-                tableT[:, c * FLIP : (c + 1) * FLIP].rearrange("d (p i) -> d p i", i=PER),
-                flip_ps[:].rearrange("d i p -> d p i"),
-            )
 
         a1 = held.tile([P, KA, N], BF16, name="a1")
         x = held.tile([P, N], BF16, name="x")

@@ -33,8 +33,8 @@ def tile_decomposableattention_b_kernel(
         offsets = held.tile([P, N // 16], U16, name="offsets")
         rows = held.tile([P, V // P, E], BF16, name="rows")
         table_blocks = table.rearrange("(b p) e -> p b e", p=P)
-        for c in range(4):
-            blocks = slice(c * 8, (c + 1) * 8)
+        for f in range(V // FLIP):
+            blocks = slice(f * (FLIP // P), (f + 1) * (FLIP // P))
             nc.sync.dma_start(rows[:, blocks, :], table_blocks[:, blocks, :])
         nc.sync.dma_start(offsets[:], offs)
 

@@ -11,13 +11,17 @@ AXIS_X = mybir.AxisListType.X
 P = 128
 V, E, HA, HC = 4096, 128, 512, 1024
 N, PIECE, BLOCK = 1536, 512, 256
-PAIRS, BLOCKS = N // PIECE, N // BLOCK
+PAIRS = N // PIECE
 KA, KC = HA // P, HC // P
+GROUPS = BLOCK // P
+LOADS = 4
 FLIP = 512
+PSUM_BANKS = 8
 
-FLOPS = 2 * N * (E * HA + HA * HA + 2 * E * HC + HC * HC) + BLOCKS * 2 * BLOCK * BLOCK * (HA + E)
+FLOPS = 2 * N * (E * HA + HA * HA + 2 * E * HC + HC * HC) + 2 * N * BLOCK * (HA + E)
 
 B1A, B2A, B1C, B2C = 0, KA, 2 * KA, 2 * KA + KC
+BIAS_COLUMNS = 2 * KA + 2 * KC
 
 
 def tile_decomposableattention_b_kernel(
@@ -28,32 +32,30 @@ def tile_decomposableattention_b_kernel(
         held = stack.enter_context(tc.tile_pool(name="held", bufs=1))
         soft = stack.enter_context(tc.tile_pool(name="soft", bufs=4))
         stage = stack.enter_context(tc.tile_pool(name="stage", bufs=4))
-        psum = stack.enter_context(tc.psum_pool(name="psum", bufs=8))
+        psum = stack.enter_context(tc.psum_pool(name="psum", bufs=PSUM_BANKS))
 
-        offsets = held.tile([P, N // 16], U16, name="offsets")
         rows = held.tile([P, V // P, E], BF16, name="rows")
-        table_blocks = table.rearrange("(b p) e -> p b e", p=P)
-        for f in range(V // FLIP):
-            blocks = slice(f * (FLIP // P), (f + 1) * (FLIP // P))
-            nc.sync.dma_start(rows[:, blocks, :], table_blocks[:, blocks, :])
+        table_slabs = table.rearrange("(slab q) e -> q slab e", q=P)
+        for load in range(LOADS):
+            slabs = slice(load * (V // P // LOADS), (load + 1) * (V // P // LOADS))
+            nc.sync.dma_start(rows[:, slabs, :], table_slabs[:, slabs, :])
+        offsets = held.tile([P, N // 16], U16, name="offsets")
         nc.sync.dma_start(offsets[:], offs)
+        w2a_sb = held.tile([P, KA, HA], BF16, name="w2a_sb")
+        nc.sync.dma_start(w2a_sb[:], w2a.rearrange("(kg q) f -> q kg f", q=P))
+        w1c_sb = held.tile([P, 2, HC], BF16, name="w1c_sb")
+        nc.sync.dma_start(w1c_sb[:], w1c.rearrange("(kg q) f -> q kg f", q=P))
+        w2c_sb = held.tile([P, KC, HC], BF16, name="w2c_sb")
+        nc.sync.dma_start(w2c_sb[:], w2c.rearrange("(kg q) f -> q kg f", q=P))
 
         w1a_sb = held.tile([P, HA], BF16, name="w1a_sb")
         nc.scalar.dma_start(w1a_sb[:], w1a)
-
         bias_rows = held.tile([P, P], F32, name="bias_rows")
         nc.vector.memset(bias_rows[:], 0.0)
-        for column, vector, count in ((B1A, b1a, KA), (B2A, b2a, KA), (B1C, b1c, KC), (B2C, b2c, KC)):
+        for column, bias_in, count in ((B1A, b1a, KA), (B2A, b2a, KA), (B1C, b1c, KC), (B2C, b2c, KC)):
             nc.scalar.dma_start(
-                bias_rows[column : column + count, :], vector.rearrange("(m p) o -> m (p o)", p=P)
+                bias_rows[column : column + count, :], bias_in.rearrange("(og q) one -> og (q one)", q=P)
             )
-
-        w2a_sb = held.tile([P, KA, HA], BF16, name="w2a_sb")
-        nc.sync.dma_start(w2a_sb[:], w2a.rearrange("(k p) m -> p k m", p=P))
-        w1c_sb = held.tile([P, 2, HC], BF16, name="w1c_sb")
-        nc.sync.dma_start(w1c_sb[:], w1c.rearrange("(k p) m -> p k m", p=P))
-        w2c_sb = held.tile([P, KC, HC], BF16, name="w2c_sb")
-        nc.sync.dma_start(w2c_sb[:], w2c.rearrange("(k p) m -> p k m", p=P))
 
         ident_bf = held.tile([P, P], BF16, name="ident_bf")
         make_identity(nc, ident_bf[:])
@@ -66,22 +68,22 @@ def tile_decomposableattention_b_kernel(
 
         turn = [0]
 
-        def next_engine_is_scalar():
+        def scalar_has_the_turn():
             turn[0] += 1
             return turn[0] % 2 == 1
 
-        def copy_out(dst, src):
-            if next_engine_is_scalar():
-                nc.scalar.copy(dst, src)
+        def copy_out(dst, bank):
+            if scalar_has_the_turn():
+                nc.scalar.copy(dst, bank)
             else:
-                nc.vector.tensor_copy(dst, src)
+                nc.vector.tensor_copy(dst, bank)
 
-        def relu_out(dst, src, bias_column):
+        def relu_out(dst, bank, bias_column):
             bias = biases[:, bias_column : bias_column + 1]
-            if next_engine_is_scalar():
-                nc.scalar.activation(dst, src, ACT.Relu, bias=bias)
+            if scalar_has_the_turn():
+                nc.scalar.activation(dst, bank, ACT.Relu, bias=bias)
             else:
-                nc.vector.tensor_scalar(dst, src, bias, 0.0, op0=ALU.add, op1=ALU.max)
+                nc.vector.tensor_scalar(dst, bank, bias, 0.0, op0=ALU.add, op1=ALU.max)
 
         tableT = held.tile([P, V], BF16, name="tableT")
         for f in range(V // FLIP):
@@ -94,138 +96,138 @@ def tile_decomposableattention_b_kernel(
 
         bias_ps = psum.tile([P, P], F32, tag="bank")
         nc.tensor.transpose(bias_ps[:], bias_rows[:], ident_f32[:])
-        biases = held.tile([P, B2C + KC], F32, name="biases")
-        nc.vector.tensor_copy(biases[:], bias_ps[:, : B2C + KC])
+        biases = held.tile([P, BIAS_COLUMNS], F32, name="biases")
+        nc.vector.tensor_copy(biases[:], bias_ps[:, :BIAS_COLUMNS])
 
         a1 = held.tile([P, KA, N], BF16, name="a1")
         x = held.tile([P, N], BF16, name="x")
-        for p in range(PAIRS):
-            cols = slice(p * PIECE, (p + 1) * PIECE)
-            looked_up = tableT[:].indirect(offsets[:, p * (PIECE // 16) : (p + 1) * (PIECE // 16)])
-            for m in range(KA):
+        for pair in range(PAIRS):
+            cols = slice(pair * PIECE, (pair + 1) * PIECE)
+            looked_up = tableT[:].indirect(offsets[:, pair * (PIECE // 16) : (pair + 1) * (PIECE // 16)])
+            for og in range(KA):
                 a1_ps = psum.tile([P, PIECE], F32, tag="bank")
-                nc.tensor.matmul(a1_ps[:], w1a_sb[:, m * P : (m + 1) * P], looked_up)
-                relu_out(a1[:, m, cols], a1_ps[:], B1A + m)
+                nc.tensor.matmul(a1_ps[:], w1a_sb[:, og * P : (og + 1) * P], looked_up)
+                relu_out(a1[:, og, cols], a1_ps[:], B1A + og)
             x_ps = psum.tile([P, PIECE], F32, tag="bank")
             nc.tensor.matmul(x_ps[:], ident_bf[:], looked_up)
             copy_out(x[:, cols], x_ps[:])
 
         xT = held.tile([P, N], BF16, name="xT")
-
-        def flip_words(p):
-            xT_ps = psum.tile([P, PIECE], BF16, tag="bank")
-            for i in range(PIECE // P):
-                group = slice(p * PIECE + i * P, p * PIECE + (i + 1) * P)
-                nc.tensor.transpose(xT_ps[:, i * P : (i + 1) * P], x[:, group], ident_bf[:])
-            copy_out(xT[:, p * PIECE : (p + 1) * PIECE], xT_ps[:])
-
         h = held.tile([P, KA, N], BF16, name="h")
-
-        def hidden(p):
-            cols = slice(p * PIECE, (p + 1) * PIECE)
-            for m in range(KA):
-                h_ps = psum.tile([P, PIECE], F32, tag="bank")
-                for k in range(KA):
-                    nc.tensor.matmul(
-                        h_ps[:], w2a_sb[:, k, m * P : (m + 1) * P], a1[:, k, cols],
-                        start=(k == 0), stop=(k == KA - 1),
-                    )
-                relu_out(h[:, m, cols], h_ps[:], B2A + m)
-
-        halves = BLOCK // P
+        ctx = held.tile([P, N], BF16, name="ctx")
+        c1 = held.tile([P, KC, N], BF16, name="c1")
         att_of = {}
         attT_of = {}
-        ctx = held.tile([P, N], BF16, name="ctx")
 
-        def scores(r):
-            theirs = slice((r ^ 1) * BLOCK, ((r ^ 1) + 1) * BLOCK)
-            sc_ps = psum.tile([P, halves, BLOCK], F32, tag="bank")
-            for g in range(halves):
-                mine = slice(r * BLOCK + g * P, r * BLOCK + (g + 1) * P)
-                for k in range(KA):
+        def flip_words(pair):
+            xT_ps = psum.tile([P, PIECE], BF16, tag="bank")
+            for i in range(PIECE // P):
+                words = slice(pair * PIECE + i * P, pair * PIECE + (i + 1) * P)
+                nc.tensor.transpose(xT_ps[:, i * P : (i + 1) * P], x[:, words], ident_bf[:])
+            copy_out(xT[:, pair * PIECE : (pair + 1) * PIECE], xT_ps[:])
+
+        def hidden(pair):
+            cols = slice(pair * PIECE, (pair + 1) * PIECE)
+            for og in range(KA):
+                h_ps = psum.tile([P, PIECE], F32, tag="bank")
+                for kg in range(KA):
                     nc.tensor.matmul(
-                        sc_ps[:, g, :], h[:, k, mine], h[:, k, theirs],
-                        start=(k == 0), stop=(k == KA - 1),
+                        h_ps[:], w2a_sb[:, kg, og * P : (og + 1) * P], a1[:, kg, cols],
+                        start=(kg == 0), stop=(kg == KA - 1),
                     )
-            neg_max = soft.tile([P, halves], F32, tag="neg_max")
+                relu_out(h[:, og, cols], h_ps[:], B2A + og)
+
+        def scores(block):
+            partner = block ^ 1
+            theirs = slice(partner * BLOCK, (partner + 1) * BLOCK)
+            sc_ps = psum.tile([P, GROUPS, BLOCK], F32, tag="bank")
+            for wg in range(GROUPS):
+                mine = slice(block * BLOCK + wg * P, block * BLOCK + (wg + 1) * P)
+                for kg in range(KA):
+                    nc.tensor.matmul(
+                        sc_ps[:, wg, :], h[:, kg, mine], h[:, kg, theirs],
+                        start=(kg == 0), stop=(kg == KA - 1),
+                    )
+            neg_max = soft.tile([P, GROUPS], F32, tag="neg_max")
             nc.vector.reduce_max(neg_max[:], sc_ps[:], axis=AXIS_X, negate=True)
-            expo = soft.tile([P, halves, BLOCK], F32, tag="expo")
-            sums = soft.tile([P, halves], F32, tag="sums")
-            for g in range(halves):
+            expo = soft.tile([P, GROUPS, BLOCK], F32, tag="expo")
+            sums = soft.tile([P, GROUPS], F32, tag="sums")
+            for wg in range(GROUPS):
                 nc.scalar.activation(
-                    expo[:, g, :], sc_ps[:, g, :], ACT.Exp,
-                    bias=neg_max[:, g : g + 1], accum_out=sums[:, g : g + 1],
+                    expo[:, wg, :], sc_ps[:, wg, :], ACT.Exp,
+                    bias=neg_max[:, wg : wg + 1], accum_out=sums[:, wg : wg + 1],
                 )
-            inverse = soft.tile([P, halves], F32, tag="inverse")
+            inverse = soft.tile([P, GROUPS], F32, tag="inverse")
             nc.vector.reciprocal(inverse[:], sums[:])
-            att = soft.tile([P, halves, BLOCK], BF16, tag="att")
-            for g in range(halves):
+            att = soft.tile([P, GROUPS, BLOCK], BF16, tag="att")
+            for wg in range(GROUPS):
                 nc.vector.tensor_scalar(
-                    att[:, g, :], expo[:, g, :], inverse[:, g : g + 1], None, op0=ALU.mult
+                    att[:, wg, :], expo[:, wg, :], inverse[:, wg : wg + 1], None, op0=ALU.mult
                 )
-            att_of[r] = att
+            att_of[block] = att
 
-        def flip_att(r):
-            att = att_of[r]
-            attT_ps = psum.tile([P, halves, BLOCK], BF16, tag="bank")
-            for u in range(halves):
-                for g in range(halves):
+        def flip_att(block):
+            att = att_of[block]
+            attT_ps = psum.tile([P, GROUPS, BLOCK], BF16, tag="bank")
+            for tg in range(GROUPS):
+                for wg in range(GROUPS):
                     nc.tensor.transpose(
-                        attT_ps[:, u, g * P : (g + 1) * P], att[:, g, u * P : (u + 1) * P], ident_bf[:]
+                        attT_ps[:, tg, wg * P : (wg + 1) * P], att[:, wg, tg * P : (tg + 1) * P], ident_bf[:]
                     )
-            attT = soft.tile([P, halves, BLOCK], BF16, tag="attT")
+            attT = soft.tile([P, GROUPS, BLOCK], BF16, tag="attT")
             copy_out(attT[:], attT_ps[:])
-            attT_of[r] = attT
+            attT_of[block] = attT
 
-        def context(r):
-            attT = attT_of[r]
+        def context(block):
+            partner = block ^ 1
+            attT = attT_of[block]
             ctx_ps = psum.tile([P, BLOCK], F32, tag="bank")
-            for u in range(halves):
-                their_group = slice((r ^ 1) * BLOCK + u * P, (r ^ 1) * BLOCK + (u + 1) * P)
+            for tg in range(GROUPS):
+                their_words = slice(partner * BLOCK + tg * P, partner * BLOCK + (tg + 1) * P)
                 nc.tensor.matmul(
-                    ctx_ps[:], xT[:, their_group], attT[:, u, :],
-                    start=(u == 0), stop=(u == halves - 1),
+                    ctx_ps[:], xT[:, their_words], attT[:, tg, :],
+                    start=(tg == 0), stop=(tg == GROUPS - 1),
                 )
-            copy_out(ctx[:, r * BLOCK : (r + 1) * BLOCK], ctx_ps[:])
+            copy_out(ctx[:, block * BLOCK : (block + 1) * BLOCK], ctx_ps[:])
 
-        c1 = held.tile([P, KC, N], BF16, name="c1")
-
-        def compare(p):
-            cols = slice(p * PIECE, (p + 1) * PIECE)
-            for m in range(KC):
+        def compare(pair):
+            cols = slice(pair * PIECE, (pair + 1) * PIECE)
+            for og in range(KC):
                 c1_ps = psum.tile([P, PIECE], F32, tag="bank")
-                nc.tensor.matmul(c1_ps[:], w1c_sb[:, 0, m * P : (m + 1) * P], x[:, cols], start=True, stop=False)
-                nc.tensor.matmul(c1_ps[:], w1c_sb[:, 1, m * P : (m + 1) * P], ctx[:, cols], start=False, stop=True)
-                relu_out(c1[:, m, cols], c1_ps[:], B1C + m)
+                nc.tensor.matmul(c1_ps[:], w1c_sb[:, 0, og * P : (og + 1) * P], x[:, cols], start=True, stop=False)
+                nc.tensor.matmul(c1_ps[:], w1c_sb[:, 1, og * P : (og + 1) * P], ctx[:, cols], start=False, stop=True)
+                relu_out(c1[:, og, cols], c1_ps[:], B1C + og)
+
+        def output(pair):
+            cols = slice(pair * PIECE, (pair + 1) * PIECE)
+            for og in range(KC):
+                out_ps = psum.tile([P, PIECE], F32, tag="bank")
+                for kg in range(KC):
+                    nc.tensor.matmul(
+                        out_ps[:], w2c_sb[:, kg, og * P : (og + 1) * P], c1[:, kg, cols],
+                        start=(kg == 0), stop=(kg == KC - 1),
+                    )
+                out_sb = stage.tile([P, PIECE], F32, tag="out_sb")
+                relu_out(out_sb[:], out_ps[:], B2C + og)
+                nc.sync.dma_start(out[og * P : (og + 1) * P, cols], out_sb[:])
 
         hidden(0)
-        for p in range(PAIRS):
-            flip_words(p)
+        for pair in range(PAIRS):
+            flip_words(pair)
         hidden(1)
         scores(0)
         scores(1)
         hidden(2)
-        for p in range(PAIRS):
-            first, second = 2 * p, 2 * p + 1
+        for pair in range(PAIRS):
+            first, second = 2 * pair, 2 * pair + 1
             flip_att(first)
             flip_att(second)
-            if p + 1 < PAIRS:
+            if pair + 1 < PAIRS:
                 scores(first + 2)
             context(first)
             context(second)
-            if p + 1 < PAIRS:
+            if pair + 1 < PAIRS:
                 scores(second + 2)
-            compare(p)
-
-        for p in range(PAIRS):
-            cols = slice(p * PIECE, (p + 1) * PIECE)
-            for m in range(KC):
-                out_ps = psum.tile([P, PIECE], F32, tag="bank")
-                for k in range(KC):
-                    nc.tensor.matmul(
-                        out_ps[:], w2c_sb[:, k, m * P : (m + 1) * P], c1[:, k, cols],
-                        start=(k == 0), stop=(k == KC - 1),
-                    )
-                out_sb = stage.tile([P, PIECE], F32, tag="out_sb")
-                relu_out(out_sb[:], out_ps[:], B2C + m)
-                nc.sync.dma_start(out[m * P : (m + 1) * P, cols], out_sb[:])
+            compare(pair)
+        for pair in range(PAIRS):
+            output(pair)

@@ -6,7 +6,6 @@ from concourse.masks import make_identity
 BF16, F32, U16 = mybir.dt.bfloat16, mybir.dt.float32, mybir.dt.uint16
 ACT = mybir.ActivationFunctionType
 ALU = mybir.AluOpType
-AXIS_X = mybir.AxisListType.X
 
 P = 128
 V, E, HA, HC = 4096, 128, 512, 1024
@@ -17,6 +16,7 @@ GROUPS = BLOCK // P
 LOADS = 4
 FLIP = 512
 PSUM_BANKS = 8
+SHIFT = 30.0
 
 FLOPS = 2 * N * (E * HA + HA * HA + 2 * E * HC + HC * HC) + 2 * N * BLOCK * (HA + E)
 
@@ -30,7 +30,7 @@ def tile_decomposableattention_b_kernel(
     nc = tc.nc
     with ExitStack() as stack:
         held = stack.enter_context(tc.tile_pool(name="held", bufs=1))
-        soft = stack.enter_context(tc.tile_pool(name="soft", bufs=4))
+        soft = stack.enter_context(tc.tile_pool(name="soft", bufs=2))
         stage = stack.enter_context(tc.tile_pool(name="stage", bufs=4))
         psum = stack.enter_context(tc.psum_pool(name="psum", bufs=PSUM_BANKS))
 
@@ -61,6 +61,8 @@ def tile_decomposableattention_b_kernel(
         make_identity(nc, ident_bf[:])
         ident_f32 = held.tile([P, P], F32, name="ident_f32")
         make_identity(nc, ident_f32[:])
+        ones = held.tile([P, P], BF16, name="ones")
+        nc.vector.memset(ones[:], 1.0)
 
         warm = held.tile([P, 1], F32, name="warm")
         nc.vector.memset(warm[:], 0.0)
@@ -116,8 +118,7 @@ def tile_decomposableattention_b_kernel(
         h = held.tile([P, KA, N], BF16, name="h")
         ctx = held.tile([P, N], BF16, name="ctx")
         c1 = held.tile([P, KC, N], BF16, name="c1")
-        att_of = {}
-        attT_of = {}
+        expo_of = {}
 
         def flip_words(pair):
             xT_ps = psum.tile([P, PIECE], BF16, tag="bank")
@@ -137,58 +138,54 @@ def tile_decomposableattention_b_kernel(
                     )
                 relu_out(h[:, og, cols], h_ps[:], B2A + og)
 
-        def scores(block):
-            partner = block ^ 1
-            theirs = slice(partner * BLOCK, (partner + 1) * BLOCK)
+        def scores(pair):
+            first, second = 2 * pair, 2 * pair + 1
+            theirs = slice(second * BLOCK, (second + 1) * BLOCK)
             sc_ps = psum.tile([P, GROUPS, BLOCK], F32, tag="bank")
             for wg in range(GROUPS):
-                mine = slice(block * BLOCK + wg * P, block * BLOCK + (wg + 1) * P)
+                mine = slice(first * BLOCK + wg * P, first * BLOCK + (wg + 1) * P)
                 for kg in range(KA):
                     nc.tensor.matmul(
                         sc_ps[:, wg, :], h[:, kg, mine], h[:, kg, theirs],
                         start=(kg == 0), stop=(kg == KA - 1),
                     )
-            neg_max = soft.tile([P, GROUPS], F32, tag="neg_max")
-            nc.vector.reduce_max(neg_max[:], sc_ps[:], axis=AXIS_X, negate=True)
-            expo = soft.tile([P, GROUPS, BLOCK], F32, tag="expo")
-            sums = soft.tile([P, GROUPS], F32, tag="sums")
-            for wg in range(GROUPS):
-                nc.scalar.activation(
-                    expo[:, wg, :], sc_ps[:, wg, :], ACT.Exp,
-                    bias=neg_max[:, wg : wg + 1], accum_out=sums[:, wg : wg + 1],
-                )
-            inverse = soft.tile([P, GROUPS], F32, tag="inverse")
-            nc.vector.reciprocal(inverse[:], sums[:])
-            att = soft.tile([P, GROUPS, BLOCK], BF16, tag="att")
-            for wg in range(GROUPS):
-                nc.vector.tensor_scalar(
-                    att[:, wg, :], expo[:, wg, :], inverse[:, wg : wg + 1], None, op0=ALU.mult
-                )
-            att_of[block] = att
+            expo = soft.tile([P, GROUPS, BLOCK], BF16, tag="expo")
+            nc.scalar.activation(expo[:], sc_ps[:], ACT.Exp, bias=-SHIFT)
+            expo_of[second] = expo
 
-        def flip_att(block):
-            att = att_of[block]
-            attT_ps = psum.tile([P, GROUPS, BLOCK], BF16, tag="bank")
+        def flip_expo(pair):
+            first, second = 2 * pair, 2 * pair + 1
+            expo = expo_of[second]
+            expoT_ps = psum.tile([P, GROUPS, BLOCK], BF16, tag="bank")
             for tg in range(GROUPS):
                 for wg in range(GROUPS):
                     nc.tensor.transpose(
-                        attT_ps[:, tg, wg * P : (wg + 1) * P], att[:, wg, tg * P : (tg + 1) * P], ident_bf[:]
+                        expoT_ps[:, tg, wg * P : (wg + 1) * P], expo[:, wg, tg * P : (tg + 1) * P], ident_bf[:]
                     )
-            attT = soft.tile([P, GROUPS, BLOCK], BF16, tag="attT")
-            copy_out(attT[:], attT_ps[:])
-            attT_of[block] = attT
+            expoT = soft.tile([P, GROUPS, BLOCK], BF16, tag="expoT")
+            copy_out(expoT[:], expoT_ps[:])
+            expo_of[first] = expoT
 
         def context(block):
             partner = block ^ 1
-            attT = attT_of[block]
-            ctx_ps = psum.tile([P, BLOCK], F32, tag="bank")
+            expo = expo_of[block]
+            ctx_ps = psum.tile([P, 2, BLOCK], F32, tag="bank")
             for tg in range(GROUPS):
                 their_words = slice(partner * BLOCK + tg * P, partner * BLOCK + (tg + 1) * P)
                 nc.tensor.matmul(
-                    ctx_ps[:], xT[:, their_words], attT[:, tg, :],
+                    ctx_ps[:, 0, :], xT[:, their_words], expo[:, tg, :],
                     start=(tg == 0), stop=(tg == GROUPS - 1),
                 )
-            copy_out(ctx[:, block * BLOCK : (block + 1) * BLOCK], ctx_ps[:])
+            for tg in range(GROUPS):
+                nc.tensor.matmul(
+                    ctx_ps[:, 1, :], ones[:], expo[:, tg, :],
+                    start=(tg == 0), stop=(tg == GROUPS - 1),
+                )
+            inverse = soft.tile([P, BLOCK], F32, tag="inverse")
+            nc.vector.reciprocal(inverse[:], ctx_ps[:, 1, :])
+            nc.vector.tensor_tensor(
+                ctx[:, block * BLOCK : (block + 1) * BLOCK], ctx_ps[:, 0, :], inverse[:], op=ALU.mult
+            )
 
         def compare(pair):
             cols = slice(pair * PIECE, (pair + 1) * PIECE)
@@ -214,20 +211,23 @@ def tile_decomposableattention_b_kernel(
         hidden(0)
         for pair in range(PAIRS):
             flip_words(pair)
-        hidden(1)
         scores(0)
+        hidden(1)
+        flip_expo(0)
+        context(1)
         scores(1)
+        context(0)
         hidden(2)
-        for pair in range(PAIRS):
-            first, second = 2 * pair, 2 * pair + 1
-            flip_att(first)
-            flip_att(second)
-            if pair + 1 < PAIRS:
-                scores(first + 2)
-            context(first)
-            context(second)
-            if pair + 1 < PAIRS:
-                scores(second + 2)
-            compare(pair)
-        for pair in range(PAIRS):
-            output(pair)
+        flip_expo(1)
+        context(3)
+        scores(2)
+        context(2)
+        compare(0)
+        flip_expo(2)
+        context(5)
+        compare(1)
+        context(4)
+        output(0)
+        compare(2)
+        output(1)
+        output(2)

@@ -16,6 +16,7 @@ GROUPS = BLOCK // P
 LOADS = 4
 FLIP = 512
 PSUM_BANKS = 8
+LAST_CUT = 4
 SHIFT = 30.0
 
 FLOPS = 2 * N * (E * HA + HA * HA + 2 * E * HC + HC * HC) + 2 * N * BLOCK * (HA + E)
@@ -31,7 +32,7 @@ def tile_decomposableattention_b_kernel(
     with ExitStack() as stack:
         held = stack.enter_context(tc.tile_pool(name="held", bufs=1))
         soft = stack.enter_context(tc.tile_pool(name="soft", bufs=2))
-        stage = stack.enter_context(tc.tile_pool(name="stage", bufs=4))
+        stage = stack.enter_context(tc.tile_pool(name="stage", bufs=4 + LAST_CUT))
         psum = stack.enter_context(tc.psum_pool(name="psum", bufs=PSUM_BANKS))
 
         rows = held.tile([P, V // P, E], BF16, name="rows")
@@ -196,17 +197,20 @@ def tile_decomposableattention_b_kernel(
                 relu_out(c1[:, og, cols], c1_ps[:], B1C + og)
 
         def output(pair):
-            cols = slice(pair * PIECE, (pair + 1) * PIECE)
             for og in range(KC):
-                out_ps = psum.tile([P, PIECE], F32, tag="bank")
-                for kg in range(KC):
-                    nc.tensor.matmul(
-                        out_ps[:], w2c_sb[:, kg, og * P : (og + 1) * P], c1[:, kg, cols],
-                        start=(kg == 0), stop=(kg == KC - 1),
-                    )
-                out_sb = stage.tile([P, PIECE], F32, tag="out_sb")
-                relu_out(out_sb[:], out_ps[:], B2C + og)
-                nc.sync.dma_start(out[og * P : (og + 1) * P, cols], out_sb[:])
+                cut = LAST_CUT if (pair == PAIRS - 1 and og == KC - 1) else 1
+                width = PIECE // cut
+                for part in range(cut):
+                    cols = slice(pair * PIECE + part * width, pair * PIECE + (part + 1) * width)
+                    out_ps = psum.tile([P, width], F32, tag="bank")
+                    for kg in range(KC):
+                        nc.tensor.matmul(
+                            out_ps[:], w2c_sb[:, kg, og * P : (og + 1) * P], c1[:, kg, cols],
+                            start=(kg == 0), stop=(kg == KC - 1),
+                        )
+                    out_sb = stage.tile([P, width], F32, tag="out_sb")
+                    relu_out(out_sb[:], out_ps[:], B2C + og)
+                    nc.sync.dma_start(out[og * P : (og + 1) * P, cols], out_sb[:])
 
         hidden(0)
         for pair in range(PAIRS):

@@ -119,7 +119,8 @@ def tile_decomposableattention_b_kernel(
         h = held.tile([P, KA, N], BF16, name="h")
         ctx = held.tile([P, N], BF16, name="ctx")
         c1 = held.tile([P, KC, N], BF16, name="c1")
-        expo_of = {}
+        weights_of = {}
+        att_of = {}
 
         def flip_words(pair):
             xT_ps = psum.tile([P, PIECE], BF16, tag="bank")
@@ -150,42 +151,64 @@ def tile_decomposableattention_b_kernel(
                         sc_ps[:, wg, :], h[:, kg, mine], h[:, kg, theirs],
                         start=(kg == 0), stop=(kg == KA - 1),
                     )
-            expo = soft.tile([P, GROUPS, BLOCK], BF16, tag="expo")
-            nc.scalar.activation(expo[:], sc_ps[:], ACT.Exp, bias=-SHIFT)
-            expo_of[second] = expo
+            expo = soft.tile([P, GROUPS, BLOCK], F32, tag="expo")
+            sums = soft.tile([P, GROUPS], F32, tag="sums")
+            for wg in range(GROUPS):
+                nc.scalar.activation(
+                    expo[:, wg, :], sc_ps[:, wg, :], ACT.Exp, bias=-SHIFT, accum_out=sums[:, wg : wg + 1]
+                )
+            rounded = soft.tile([P, GROUPS, BLOCK], BF16, tag="rounded")
+            nc.vector.tensor_copy(rounded[:], expo[:])
+            weights_of[second] = rounded
+            inverse = soft.tile([P, GROUPS], F32, tag="inverse")
+            nc.vector.reciprocal(inverse[:], sums[:])
+            att = soft.tile([P, GROUPS, BLOCK], BF16, tag="att")
+            for wg in range(GROUPS):
+                nc.vector.tensor_scalar(
+                    att[:, wg, :], expo[:, wg, :], inverse[:, wg : wg + 1], None, op0=ALU.mult
+                )
+            att_of[pair] = att
 
-        def flip_expo(pair):
-            first, second = 2 * pair, 2 * pair + 1
-            expo = expo_of[second]
-            expoT_ps = psum.tile([P, GROUPS, BLOCK], BF16, tag="bank")
+        def flip_att(pair):
+            att = att_of[pair]
+            attT_ps = psum.tile([P, GROUPS, BLOCK], BF16, tag="bank")
             for tg in range(GROUPS):
                 for wg in range(GROUPS):
                     nc.tensor.transpose(
-                        expoT_ps[:, tg, wg * P : (wg + 1) * P], expo[:, wg, tg * P : (tg + 1) * P], ident_bf[:]
+                        attT_ps[:, tg, wg * P : (wg + 1) * P], att[:, wg, tg * P : (tg + 1) * P], ident_bf[:]
                     )
-            expoT = soft.tile([P, GROUPS, BLOCK], BF16, tag="expoT")
-            copy_out(expoT[:], expoT_ps[:])
-            expo_of[first] = expoT
+            attT = soft.tile([P, GROUPS, BLOCK], BF16, tag="attT")
+            copy_out(attT[:], attT_ps[:])
+            weights_of[2 * pair] = attT
 
-        def context(block):
+        def weighted_words(bank, block):
             partner = block ^ 1
-            expo = expo_of[block]
-            ctx_ps = psum.tile([P, 2, BLOCK], F32, tag="bank")
             for tg in range(GROUPS):
                 their_words = slice(partner * BLOCK + tg * P, partner * BLOCK + (tg + 1) * P)
                 nc.tensor.matmul(
-                    ctx_ps[:, 0, :], xT[:, their_words], expo[:, tg, :],
+                    bank, xT[:, their_words], weights_of[block][:, tg, :],
                     start=(tg == 0), stop=(tg == GROUPS - 1),
                 )
+
+        def context_of_first(pair):
+            block = 2 * pair
+            ctx_ps = psum.tile([P, BLOCK], F32, tag="bank")
+            weighted_words(ctx_ps[:], block)
+            copy_out(ctx[:, block * BLOCK : (block + 1) * BLOCK], ctx_ps[:])
+
+        def context_of_second(pair):
+            block = 2 * pair + 1
+            ctx_ps = psum.tile([P, 2, BLOCK], F32, tag="bank")
+            weighted_words(ctx_ps[:, 0, :], block)
             for tg in range(GROUPS):
                 nc.tensor.matmul(
-                    ctx_ps[:, 1, :], ones[:], expo[:, tg, :],
+                    ctx_ps[:, 1, :], ones[:], weights_of[block][:, tg, :],
                     start=(tg == 0), stop=(tg == GROUPS - 1),
                 )
-            inverse = soft.tile([P, BLOCK], F32, tag="inverse")
-            nc.vector.reciprocal(inverse[:], ctx_ps[:, 1, :])
+            divisor = soft.tile([P, BLOCK], F32, tag="divisor")
+            nc.vector.reciprocal(divisor[:], ctx_ps[:, 1, :])
             nc.vector.tensor_tensor(
-                ctx[:, block * BLOCK : (block + 1) * BLOCK], ctx_ps[:, 0, :], inverse[:], op=ALU.mult
+                ctx[:, block * BLOCK : (block + 1) * BLOCK], ctx_ps[:, 0, :], divisor[:], op=ALU.mult
             )
 
         def compare(pair):
@@ -217,20 +240,20 @@ def tile_decomposableattention_b_kernel(
             flip_words(pair)
         scores(0)
         hidden(1)
-        flip_expo(0)
-        context(1)
+        flip_att(0)
+        context_of_second(0)
         scores(1)
-        context(0)
+        context_of_first(0)
         hidden(2)
-        flip_expo(1)
-        context(3)
+        flip_att(1)
+        context_of_second(1)
         scores(2)
-        context(2)
+        context_of_first(1)
         compare(0)
-        flip_expo(2)
-        context(5)
+        flip_att(2)
+        context_of_second(2)
         compare(1)
-        context(4)
+        context_of_first(2)
         output(0)
         compare(2)
         output(1)

@@ -42,6 +42,8 @@ def tile_decomposableattention_b_kernel(
             nc.sync.dma_start(rows[:, slabs, :], table_slabs[:, slabs, :])
         offsets = held.tile([P, N // 16], U16, name="offsets")
         nc.sync.dma_start(offsets[:], offs)
+        w1a_sb = held.tile([P, HA], BF16, name="w1a_sb")
+        nc.sync.dma_start(w1a_sb[:], w1a)
         w2a_sb = held.tile([P, KA, HA], BF16, name="w2a_sb")
         nc.sync.dma_start(w2a_sb[:], w2a.rearrange("(kg q) f -> q kg f", q=P))
         w1c_sb = held.tile([P, 2, HC], BF16, name="w1c_sb")
@@ -49,8 +51,6 @@ def tile_decomposableattention_b_kernel(
         w2c_sb = held.tile([P, KC, HC], BF16, name="w2c_sb")
         nc.sync.dma_start(w2c_sb[:], w2c.rearrange("(kg q) f -> q kg f", q=P))
 
-        w1a_sb = held.tile([P, HA], BF16, name="w1a_sb")
-        nc.scalar.dma_start(w1a_sb[:], w1a)
         bias_rows = held.tile([P, P], F32, name="bias_rows")
         nc.vector.memset(bias_rows[:], 0.0)
         for column, bias_in, count in ((B1A, b1a, KA), (B2A, b2a, KA), (B1C, b1c, KC), (B2C, b2c, KC)):
@@ -104,16 +104,19 @@ def tile_decomposableattention_b_kernel(
 
         a1 = held.tile([P, KA, N], BF16, name="a1")
         x = held.tile([P, N], BF16, name="x")
+
+        def looked_up(pair):
+            return tableT[:].indirect(offsets[:, pair * (PIECE // 16) : (pair + 1) * (PIECE // 16)])
+
         for pair in range(PAIRS):
-            cols = slice(pair * PIECE, (pair + 1) * PIECE)
-            looked_up = tableT[:].indirect(offsets[:, pair * (PIECE // 16) : (pair + 1) * (PIECE // 16)])
+            x_ps = psum.tile([P, PIECE], F32, tag="bank")
+            nc.tensor.matmul(x_ps[:], ident_bf[:], looked_up(pair))
+            copy_out(x[:, pair * PIECE : (pair + 1) * PIECE], x_ps[:])
+        for pair in range(PAIRS):
             for og in range(KA):
                 a1_ps = psum.tile([P, PIECE], F32, tag="bank")
-                nc.tensor.matmul(a1_ps[:], w1a_sb[:, og * P : (og + 1) * P], looked_up)
-                relu_out(a1[:, og, cols], a1_ps[:], B1A + og)
-            x_ps = psum.tile([P, PIECE], F32, tag="bank")
-            nc.tensor.matmul(x_ps[:], ident_bf[:], looked_up)
-            copy_out(x[:, cols], x_ps[:])
+                nc.tensor.matmul(a1_ps[:], w1a_sb[:, og * P : (og + 1) * P], looked_up(pair))
+                relu_out(a1[:, og, pair * PIECE : (pair + 1) * PIECE], a1_ps[:], B1A + og)
 
         xT = held.tile([P, N], BF16, name="xT")
         h = held.tile([P, KA, N], BF16, name="h")

@@ -14,7 +14,8 @@ PAIRS = N // PIECE
 KA, KC = HA // P, HC // P
 GROUPS = BLOCK // P
 LOADS = 4
-FLIP = 512
+RUN = 4
+FLIP = RUN * P
 PSUM_BANKS = 8
 LAST_CUT = 4
 SHIFT = 30.0
@@ -35,11 +36,11 @@ def tile_decomposableattention_b_kernel(
         stage = stack.enter_context(tc.tile_pool(name="stage", bufs=4 + LAST_CUT))
         psum = stack.enter_context(tc.psum_pool(name="psum", bufs=PSUM_BANKS))
 
-        rows = held.tile([P, V // P, E], BF16, name="rows")
-        table_slabs = table.rearrange("(slab q) e -> q slab e", q=P)
+        rows = held.tile([P, V // FLIP, RUN, E], BF16, name="rows")
+        table_runs = table.rearrange("(f q r) e -> q f r e", q=P, r=RUN)
         for load in range(LOADS):
-            slabs = slice(load * (V // P // LOADS), (load + 1) * (V // P // LOADS))
-            nc.sync.dma_start(rows[:, slabs, :], table_slabs[:, slabs, :])
+            flips = slice(load * (V // FLIP // LOADS), (load + 1) * (V // FLIP // LOADS))
+            nc.sync.dma_start(rows[:, flips, :, :], table_runs[:, flips, :, :])
         offsets = held.tile([P, N // 16], U16, name="offsets")
         nc.sync.dma_start(offsets[:], offs)
         w1a_sb = held.tile([P, HA], BF16, name="w1a_sb")
@@ -90,12 +91,13 @@ def tile_decomposableattention_b_kernel(
 
         tableT = held.tile([P, V], BF16, name="tableT")
         for f in range(V // FLIP):
-            flip_ps = psum.tile([P, FLIP], BF16, tag="bank")
-            for i in range(FLIP // P):
-                nc.tensor.transpose(
-                    flip_ps[:, i * P : (i + 1) * P], rows[:, f * (FLIP // P) + i, :], ident_bf[:]
-                )
-            copy_out(tableT[:, f * FLIP : (f + 1) * FLIP], flip_ps[:])
+            flip_ps = psum.tile([P, RUN, P], BF16, tag="bank")
+            for r in range(RUN):
+                nc.tensor.transpose(flip_ps[:, r, :], rows[:, f, r, :], ident_bf[:])
+            copy_out(
+                tableT[:, f * FLIP : (f + 1) * FLIP].rearrange("d (q r) -> d q r", r=RUN),
+                flip_ps[:].rearrange("d r q -> d q r"),
+            )
 
         bias_ps = psum.tile([P, P], F32, tag="bank")
         nc.tensor.transpose(bias_ps[:], bias_rows[:], ident_f32[:])

@@ -18,6 +18,7 @@ RUN = 4
 FLIP = RUN * P
 PSUM_BANKS = 8
 LAST_CUT = 4
+ONES = 2
 SHIFT = 30.0
 
 FLOPS = 2 * N * (E * HA + HA * HA + 2 * E * HC + HC * HC) + 2 * N * BLOCK * (HA + E)
@@ -63,8 +64,6 @@ def tile_decomposableattention_b_kernel(
         make_identity(nc, ident_bf[:])
         ident_f32 = held.tile([P, P], F32, name="ident_f32")
         make_identity(nc, ident_f32[:])
-        ones = held.tile([P, P], BF16, name="ones")
-        nc.vector.memset(ones[:], 1.0)
 
         warm = held.tile([P, 1], F32, name="warm")
         nc.vector.memset(warm[:], 0.0)
@@ -120,19 +119,22 @@ def tile_decomposableattention_b_kernel(
                 nc.tensor.matmul(a1_ps[:], w1a_sb[:, og * P : (og + 1) * P], looked_up(pair))
                 relu_out(a1[:, og, pair * PIECE : (pair + 1) * PIECE], a1_ps[:], B1A + og)
 
-        xT = held.tile([P, N], BF16, name="xT")
+        xT = held.tile([P, N // P, E + ONES], BF16, name="xT")
+        nc.vector.memset(xT[:], 1.0)
         h = held.tile([P, KA, N], BF16, name="h")
         ctx = held.tile([P, N], BF16, name="ctx")
         c1 = held.tile([P, KC, N], BF16, name="c1")
         weights_of = {}
         att_of = {}
+        ctxT_of = {}
 
         def flip_words(pair):
             xT_ps = psum.tile([P, PIECE], BF16, tag="bank")
             for i in range(PIECE // P):
                 words = slice(pair * PIECE + i * P, pair * PIECE + (i + 1) * P)
                 nc.tensor.transpose(xT_ps[:, i * P : (i + 1) * P], x[:, words], ident_bf[:])
-            copy_out(xT[:, pair * PIECE : (pair + 1) * PIECE], xT_ps[:])
+            groups = slice(pair * (PIECE // P), (pair + 1) * (PIECE // P))
+            copy_out(xT[:, groups, :E], xT_ps[:].rearrange("t (w d) -> t w d", d=E))
 
         def hidden(pair):
             cols = slice(pair * PIECE, (pair + 1) * PIECE)
@@ -186,35 +188,40 @@ def tile_decomposableattention_b_kernel(
             copy_out(attT[:], attT_ps[:])
             weights_of[2 * pair] = attT
 
-        def weighted_words(bank, block):
-            partner = block ^ 1
+        def context_of_first(pair):
+            block, partner = 2 * pair, 2 * pair + 1
+            ctx_ps = psum.tile([P, BLOCK], F32, tag="bank")
             for tg in range(GROUPS):
-                their_words = slice(partner * BLOCK + tg * P, partner * BLOCK + (tg + 1) * P)
                 nc.tensor.matmul(
-                    bank, xT[:, their_words], weights_of[block][:, tg, :],
+                    ctx_ps[:], xT[:, partner * GROUPS + tg, :E], weights_of[block][:, tg, :],
                     start=(tg == 0), stop=(tg == GROUPS - 1),
                 )
-
-        def context_of_first(pair):
-            block = 2 * pair
-            ctx_ps = psum.tile([P, BLOCK], F32, tag="bank")
-            weighted_words(ctx_ps[:], block)
             copy_out(ctx[:, block * BLOCK : (block + 1) * BLOCK], ctx_ps[:])
 
         def context_of_second(pair):
-            block = 2 * pair + 1
-            ctx_ps = psum.tile([P, 2, BLOCK], F32, tag="bank")
-            weighted_words(ctx_ps[:, 0, :], block)
+            block, partner = 2 * pair + 1, 2 * pair
+            ctxT_ps = psum.tile([P, GROUPS, E + ONES], F32, tag="bank")
             for tg in range(GROUPS):
-                nc.tensor.matmul(
-                    ctx_ps[:, 1, :], ones[:], weights_of[block][:, tg, :],
-                    start=(tg == 0), stop=(tg == GROUPS - 1),
+                for wg in range(GROUPS):
+                    nc.tensor.matmul(
+                        ctxT_ps[:, tg, :], weights_of[block][:, wg, tg * P : (tg + 1) * P], xT[:, partner * GROUPS + wg, :],
+                        start=(wg == 0), stop=(wg == GROUPS - 1),
+                    )
+            divisor = soft.tile([P, GROUPS], F32, tag="divisor")
+            nc.vector.reciprocal(divisor[:], ctxT_ps[:, :, E])
+            ctxT = soft.tile([P, GROUPS, E], BF16, tag="ctxT")
+            for tg in range(GROUPS):
+                nc.vector.tensor_scalar(
+                    ctxT[:, tg, :], ctxT_ps[:, tg, :E], divisor[:, tg : tg + 1], None, op0=ALU.mult
                 )
-            divisor = soft.tile([P, BLOCK], F32, tag="divisor")
-            nc.vector.reciprocal(divisor[:], ctx_ps[:, 1, :])
-            nc.vector.tensor_tensor(
-                ctx[:, block * BLOCK : (block + 1) * BLOCK], ctx_ps[:, 0, :], divisor[:], op=ALU.mult
-            )
+            ctxT_of[pair] = ctxT
+
+        def flip_context(pair):
+            block = 2 * pair + 1
+            ctx_ps = psum.tile([P, BLOCK], BF16, tag="bank")
+            for tg in range(GROUPS):
+                nc.tensor.transpose(ctx_ps[:, tg * P : (tg + 1) * P], ctxT_of[pair][:, tg, :], ident_bf[:])
+            copy_out(ctx[:, block * BLOCK : (block + 1) * BLOCK], ctx_ps[:])
 
         def compare(pair):
             cols = slice(pair * PIECE, (pair + 1) * PIECE)
@@ -249,16 +256,19 @@ def tile_decomposableattention_b_kernel(
         context_of_second(0)
         scores(1)
         context_of_first(0)
+        flip_context(0)
         hidden(2)
         flip_att(1)
         context_of_second(1)
         scores(2)
         context_of_first(1)
+        flip_context(1)
         compare(0)
         flip_att(2)
         context_of_second(2)
         compare(1)
         context_of_first(2)
+        flip_context(2)
         output(0)
         compare(2)
         output(1)

from contextlib import ExitStack

import concourse.mybir as mybir
from concourse.masks import make_identity

BF16, F32, U16 = mybir.dt.bfloat16, mybir.dt.float32, mybir.dt.uint16
ACT = mybir.ActivationFunctionType
ALU = mybir.AluOpType

P = 128
V, E, HA, HC = 4096, 128, 512, 1024
N, PIECE, BLOCK = 1536, 512, 256
PAIRS = N // PIECE
KA, KC = HA // P, HC // P
GROUPS = BLOCK // P
LOADS = 4
RUN = 4
FLIP = RUN * P
PSUM_BANKS = 8
LAST_CUT = 4
ONES = 2
SHIFT = 30.0

FLOPS = 2 * N * (E * HA + HA * HA + 2 * E * HC + HC * HC) + 2 * N * BLOCK * (HA + E)

B1A, B2A, B1C, B2C = 0, KA, 2 * KA, 2 * KA + KC
BIAS_COLUMNS = 2 * KA + 2 * KC


def tile_decomposableattention_b_kernel(
    tc, table, w1a, b1a, w2a, b2a, w1c, b1c, w2c, b2c, offs, out
):
    nc = tc.nc
    with ExitStack() as stack:
        held = stack.enter_context(tc.tile_pool(name="held", bufs=1))
        soft = stack.enter_context(tc.tile_pool(name="soft", bufs=2))
        stage = stack.enter_context(tc.tile_pool(name="stage", bufs=4 + LAST_CUT))
        psum = stack.enter_context(tc.psum_pool(name="psum", bufs=PSUM_BANKS))

        rows = held.tile([P, V // FLIP, RUN, E], BF16, name="rows")
        table_runs = table.rearrange("(f q r) e -> q f r e", q=P, r=RUN)
        for load in range(LOADS):
            flips = slice(load * (V // FLIP // LOADS), (load + 1) * (V // FLIP // LOADS))
            nc.sync.dma_start(rows[:, flips, :, :], table_runs[:, flips, :, :])
        offsets = held.tile([P, N // 16], U16, name="offsets")
        nc.sync.dma_start(offsets[:], offs)
        w1a_sb = held.tile([P, HA], BF16, name="w1a_sb")
        nc.sync.dma_start(w1a_sb[:], w1a)
        w2a_sb = held.tile([P, KA, HA], BF16, name="w2a_sb")
        nc.sync.dma_start(w2a_sb[:], w2a.rearrange("(kg q) f -> q kg f", q=P))
        w1c_sb = held.tile([P, 2, HC], BF16, name="w1c_sb")
        nc.sync.dma_start(w1c_sb[:], w1c.rearrange("(kg q) f -> q kg f", q=P))
        w2c_sb = held.tile([P, KC, HC], BF16, name="w2c_sb")
        nc.sync.dma_start(w2c_sb[:], w2c.rearrange("(kg q) f -> q kg f", q=P))

        bias_rows = held.tile([P, P], F32, name="bias_rows")
        nc.vector.memset(bias_rows[:], 0.0)
        for column, bias_in, count in ((B1A, b1a, KA), (B2A, b2a, KA), (B1C, b1c, KC), (B2C, b2c, KC)):
            nc.scalar.dma_start(
                bias_rows[column : column + count, :], bias_in.rearrange("(og q) one -> og (q one)", q=P)
            )

        ident_bf = held.tile([P, P], BF16, name="ident_bf")
        make_identity(nc, ident_bf[:])
        ident_f32 = held.tile([P, P], F32, name="ident_f32")
        make_identity(nc, ident_f32[:])

        warm = held.tile([P, 1], F32, name="warm")
        nc.vector.memset(warm[:], 0.0)
        nc.scalar.activation(warm[:], warm[:], ACT.Exp)

        turn = [0]

        def scalar_has_the_turn():
            turn[0] += 1
            return turn[0] % 2 == 1

        def copy_out(dst, bank):
            if scalar_has_the_turn():
                nc.scalar.copy(dst, bank)
            else:
                nc.vector.tensor_copy(dst, bank)

        def relu_out(dst, bank, bias_column):
            bias = biases[:, bias_column : bias_column + 1]
            if scalar_has_the_turn():
                nc.scalar.activation(dst, bank, ACT.Relu, bias=bias)
            else:
                nc.vector.tensor_scalar(dst, bank, bias, 0.0, op0=ALU.add, op1=ALU.max)

        tableT = held.tile([P, V], BF16, name="tableT")
        for f in range(V // FLIP):
            flip_ps = psum.tile([P, RUN, P], BF16, tag="bank")
            for r in range(RUN):
                nc.tensor.transpose(flip_ps[:, r, :], rows[:, f, r, :], ident_bf[:])
            copy_out(
                tableT[:, f * FLIP : (f + 1) * FLIP].rearrange("d (q r) -> d q r", r=RUN),
                flip_ps[:].rearrange("d r q -> d q r"),
            )

        bias_ps = psum.tile([P, P], F32, tag="bank")
        nc.tensor.transpose(bias_ps[:], bias_rows[:], ident_f32[:])
        biases = held.tile([P, BIAS_COLUMNS], F32, name="biases")
        nc.vector.tensor_copy(biases[:], bias_ps[:, :BIAS_COLUMNS])

        a1 = held.tile([P, KA, N], BF16, name="a1")
        x = held.tile([P, N], BF16, name="x")

        def looked_up(pair):
            return tableT[:].indirect(offsets[:, pair * (PIECE // 16) : (pair + 1) * (PIECE // 16)])

        for pair in range(PAIRS):
            x_ps = psum.tile([P, PIECE], F32, tag="bank")
            nc.tensor.matmul(x_ps[:], ident_bf[:], looked_up(pair))
            copy_out(x[:, pair * PIECE : (pair + 1) * PIECE], x_ps[:])
        for pair in range(PAIRS):
            for og in range(KA):
                a1_ps = psum.tile([P, PIECE], F32, tag="bank")
                nc.tensor.matmul(a1_ps[:], w1a_sb[:, og * P : (og + 1) * P], looked_up(pair))
                relu_out(a1[:, og, pair * PIECE : (pair + 1) * PIECE], a1_ps[:], B1A + og)

        xT = held.tile([P, N // P, E + ONES], BF16, name="xT")
        nc.vector.memset(xT[:], 1.0)
        h = held.tile([P, KA, N], BF16, name="h")
        ctx = held.tile([P, N], BF16, name="ctx")
        c1 = held.tile([P, KC, N], BF16, name="c1")
        weights_of = {}
        att_of = {}
        ctxT_of = {}

        def flip_words(pair):
            xT_ps = psum.tile([P, PIECE], BF16, tag="bank")
            for i in range(PIECE // P):
                words = slice(pair * PIECE + i * P, pair * PIECE + (i + 1) * P)
                nc.tensor.transpose(xT_ps[:, i * P : (i + 1) * P], x[:, words], ident_bf[:])
            groups = slice(pair * (PIECE // P), (pair + 1) * (PIECE // P))
            copy_out(xT[:, groups, :E], xT_ps[:].rearrange("t (w d) -> t w d", d=E))

        def hidden(pair):
            cols = slice(pair * PIECE, (pair + 1) * PIECE)
            for og in range(KA):
                h_ps = psum.tile([P, PIECE], F32, tag="bank")
                for kg in range(KA):
                    nc.tensor.matmul(
                        h_ps[:], w2a_sb[:, kg, og * P : (og + 1) * P], a1[:, kg, cols],
                        start=(kg == 0), stop=(kg == KA - 1),
                    )
                relu_out(h[:, og, cols], h_ps[:], B2A + og)

        def scores(pair):
            first, second = 2 * pair, 2 * pair + 1
            theirs = slice(second * BLOCK, (second + 1) * BLOCK)
            sc_ps = psum.tile([P, GROUPS, BLOCK], F32, tag="bank")
            for wg in range(GROUPS):
                mine = slice(first * BLOCK + wg * P, first * BLOCK + (wg + 1) * P)
                for kg in range(KA):
                    nc.tensor.matmul(
                        sc_ps[:, wg, :], h[:, kg, mine], h[:, kg, theirs],
                        start=(kg == 0), stop=(kg == KA - 1),
                    )
            expo = soft.tile([P, GROUPS, BLOCK], F32, tag="expo")
            sums = soft.tile([P, GROUPS], F32, tag="sums")
            for wg in range(GROUPS):
                nc.scalar.activation(
                    expo[:, wg, :], sc_ps[:, wg, :], ACT.Exp, bias=-SHIFT, accum_out=sums[:, wg : wg + 1]
                )
            rounded = soft.tile([P, GROUPS, BLOCK], BF16, tag="rounded")
            nc.vector.tensor_copy(rounded[:], expo[:])
            weights_of[second] = rounded
            inverse = soft.tile([P, GROUPS], F32, tag="inverse")
            nc.vector.reciprocal(inverse[:], sums[:])
            att = soft.tile([P, GROUPS, BLOCK], BF16, tag="att")
            for wg in range(GROUPS):
                nc.vector.tensor_scalar(
                    att[:, wg, :], expo[:, wg, :], inverse[:, wg : wg + 1], None, op0=ALU.mult
                )
            att_of[pair] = att

        def flip_att(pair):
            att = att_of[pair]
            attT_ps = psum.tile([P, GROUPS, BLOCK], BF16, tag="bank")
            for tg in range(GROUPS):
                for wg in range(GROUPS):
                    nc.tensor.transpose(
                        attT_ps[:, tg, wg * P : (wg + 1) * P], att[:, wg, tg * P : (tg + 1) * P], ident_bf[:]
                    )
            attT = soft.tile([P, GROUPS, BLOCK], BF16, tag="attT")
            copy_out(attT[:], attT_ps[:])
            weights_of[2 * pair] = attT

        def context_of_first(pair):
            block, partner = 2 * pair, 2 * pair + 1
            ctx_ps = psum.tile([P, BLOCK], F32, tag="bank")
            for tg in range(GROUPS):
                nc.tensor.matmul(
                    ctx_ps[:], xT[:, partner * GROUPS + tg, :E], weights_of[block][:, tg, :],
                    start=(tg == 0), stop=(tg == GROUPS - 1),
                )
            copy_out(ctx[:, block * BLOCK : (block + 1) * BLOCK], ctx_ps[:])

        def context_of_second(pair):
            block, partner = 2 * pair + 1, 2 * pair
            ctxT_ps = psum.tile([P, GROUPS, E + ONES], F32, tag="bank")
            for tg in range(GROUPS):
                for wg in range(GROUPS):
                    nc.tensor.matmul(
                        ctxT_ps[:, tg, :], weights_of[block][:, wg, tg * P : (tg + 1) * P], xT[:, partner * GROUPS + wg, :],
                        start=(wg == 0), stop=(wg == GROUPS - 1),
                    )
            divisor = soft.tile([P, GROUPS], F32, tag="divisor")
            nc.vector.reciprocal(divisor[:], ctxT_ps[:, :, E])
            ctxT = soft.tile([P, GROUPS, E], BF16, tag="ctxT")
            for tg in range(GROUPS):
                nc.vector.tensor_scalar(
                    ctxT[:, tg, :], ctxT_ps[:, tg, :E], divisor[:, tg : tg + 1], None, op0=ALU.mult
                )
            ctxT_of[pair] = ctxT

        def flip_context(pair):
            block = 2 * pair + 1
            ctx_ps = psum.tile([P, BLOCK], BF16, tag="bank")
            for tg in range(GROUPS):
                nc.tensor.transpose(ctx_ps[:, tg * P : (tg + 1) * P], ctxT_of[pair][:, tg, :], ident_bf[:])
            copy_out(ctx[:, block * BLOCK : (block + 1) * BLOCK], ctx_ps[:])

        def compare(pair):
            cols = slice(pair * PIECE, (pair + 1) * PIECE)
            for og in range(KC):
                c1_ps = psum.tile([P, PIECE], F32, tag="bank")
                nc.tensor.matmul(c1_ps[:], w1c_sb[:, 0, og * P : (og + 1) * P], x[:, cols], start=True, stop=False)
                nc.tensor.matmul(c1_ps[:], w1c_sb[:, 1, og * P : (og + 1) * P], ctx[:, cols], start=False, stop=True)
                relu_out(c1[:, og, cols], c1_ps[:], B1C + og)

        def output(pair):
            for og in range(KC):
                cut = LAST_CUT if (pair == PAIRS - 1 and og == KC - 1) else 1
                width = PIECE // cut
                for part in range(cut):
                    cols = slice(pair * PIECE + part * width, pair * PIECE + (part + 1) * width)
                    out_ps = psum.tile([P, width], F32, tag="bank")
                    for kg in range(KC):
                        nc.tensor.matmul(
                            out_ps[:], w2c_sb[:, kg, og * P : (og + 1) * P], c1[:, kg, cols],
                            start=(kg == 0), stop=(kg == KC - 1),
                        )
                    out_sb = stage.tile([P, width], F32, tag="out_sb")
                    relu_out(out_sb[:], out_ps[:], B2C + og)
                    nc.sync.dma_start(out[og * P : (og + 1) * P, cols], out_sb[:])

        hidden(0)
        for pair in range(PAIRS):
            flip_words(pair)
        scores(0)
        hidden(1)
        flip_att(0)
        context_of_second(0)
        scores(1)
        context_of_first(0)
        flip_context(0)
        hidden(2)
        flip_att(1)
        context_of_second(1)
        scores(2)
        context_of_first(1)
        flip_context(1)
        compare(0)
        flip_att(2)
        context_of_second(2)
        compare(1)
        context_of_first(2)
        flip_context(2)
        output(0)
        compare(2)
        output(1)
        output(2)
